import numpy as np
import ml_dtypes


def mxq(x, axis, fmt="e4m3"):
    dtype, down = {"e4m3": (ml_dtypes.float8_e4m3fn, 7), "e5m2": (ml_dtypes.float8_e5m2, 14)}[fmt]
    v = np.moveaxis(np.asarray(x, np.float32).astype(ml_dtypes.bfloat16).astype(np.float64), axis, -1)
    blocks = v.reshape(v.shape[:-1] + (-1, 32))
    amax = np.abs(blocks).max(-1, keepdims=True)
    byte = np.maximum(np.where(amax > 0, np.frexp(amax)[1] - 1 + 127, 0) - down, 1)
    scale = np.exp2(byte - 127.0)
    codes = (blocks / scale).astype(np.float32).astype(dtype).astype(np.float64)
    return np.moveaxis((codes * scale).reshape(v.shape), -1, axis)


WIDE = False


def mx_kscale(k):
    if not WIDE:
        return np.ones(k)
    levels = np.array([10, -10, 5, -5, 0])
    a = np.random.permutation(np.resize(levels, k // 512 * 4)).reshape(k // 512, 4)
    idx = np.arange(k)
    return np.exp2(a[idx // 512, idx % 128 // 32])


BF16 = ml_dtypes.bfloat16


def bf(x):
    return np.asarray(x, np.float32).astype(BF16)


def f64(x):
    return np.asarray(x).astype(np.float64)


N, H, W, K = 512, 2048, 8, 512
TAU = 1.0


def silu(v):
    return v / (1.0 + np.exp(-v))


def softmax_last(v):
    e = np.exp(v - v.max(-1, keepdims=True))
    return e / e.sum(-1, keepdims=True)


def setup_inputs():
    s = np.tile(mx_kscale(K), W)
    return {"x": bf(np.random.standard_normal((N, W * K)) * s),
            "template_flat": bf(np.random.standard_normal((H, W * K)) / np.sqrt(K) / s)}


def reference(x, template_flat):
    n = x.shape[0]
    h = template_flat.shape[0]
    xw = f64(x).reshape(n, W, K)
    tw = f64(template_flat).reshape(h, W, K)
    xq = mxq(xw, 2, "e4m3")
    tq = mxq(tw, 2, "e4m3")
    s = (xq.transpose(1, 0, 2) @ tq.transpose(1, 2, 0)).transpose(1, 2, 0)
    gate = softmax_last(s / TAU)
    return np.sum(gate * silu(s), axis=-1)

@@ -1,0 +1,218 @@
+from contextlib import ExitStack
+
+import concourse.mybir as mybir
+from concourse.masks import make_identity
+
+FP8X4 = mybir.dt.float8_e4m3fn_x4
+BF16 = mybir.dt.bfloat16
+F32 = mybir.dt.float32
+U32 = mybir.dt.uint32
+U8 = mybir.dt.uint8
+ACT = mybir.ActivationFunctionType
+ALU = mybir.AluOpType
+
+P = 128
+N, H, W, K = 512, 2048, 8, 512
+FLOPS = 2 * N * H * W * K
+
+NC = 256
+ROUNDS = (H // P) * (N // NC)
+BANKS = 4
+PINNED = False
+
+
+def tile_dendriticlayersilu_ffn_kernel(tc, x, template_flat, out):
+    nc = tc.nc
+    with ExitStack() as ctx:
+        if PINNED:
+            ctx.enter_context(tc.manual_schedule())
+        const = ctx.enter_context(tc.tile_pool(name="const", bufs=1))
+        raw_pool = ctx.enter_context(tc.tile_pool(name="raw", bufs=6))
+        grp_pool = ctx.enter_context(tc.tile_pool(name="grp", bufs=2))
+        tq_pool = ctx.enter_context(tc.tile_pool(name="tq", bufs=3))
+        t_pool = ctx.enter_context(tc.tile_pool(name="tanh", bufs=6))
+        u_pool = ctx.enter_context(tc.tile_pool(name="u", bufs=12))
+        y_pool = ctx.enter_context(tc.tile_pool(name="y", bufs=12))
+        m_pool = ctx.enter_context(tc.tile_pool(name="m", bufs=2))
+        ps_s = ctx.enter_context(tc.psum_pool(name="ps_s", bufs=5))
+        ps_za = ctx.enter_context(tc.psum_pool(name="ps_za", bufs=1))
+        ps_tp = ctx.enter_context(tc.psum_pool(name="ps_tp", bufs=2))
+
+        ident = const.tile([P, P], F32, name="ident")
+        make_identity(nc, ident[:])
+        xq = const.tile([P, W * N], U32, name="xq", align_bytes=64)
+        xs = const.tile([P, W * N], U8, name="xs", align_bytes=64)
+        out_sb = const.tile([P, N // P, H], F32, name="out_sb")
+
+        blocks = [("x", 0), ("x", 1), ("t", 0), ("x", 2), ("x", 3)] + [("t", i) for i in range(1, H // P)]
+        raw = {}
+        grp = {}
+        tq = {}
+        ts = {}
+
+        def load(i):
+            kind, idx = blocks[i]
+            src = x if kind == "x" else template_flat
+            r = raw_pool.tile([P, W * K], BF16, name="raw")
+            nc.sync.dma_start(out=r[:], in_=src[idx * P : (idx + 1) * P, :])
+            raw[i] = r
+
+        def transposes(i, j, engine):
+            if j == 0:
+                grp[i] = grp_pool.tile([P, W * K], BF16, name="grp", align_bytes=64)
+            words = raw[i][:].bitcast(F32)
+            tp = ps_tp.tile([P, 512], F32, name="tp")
+            for q in range(4):
+                nc.tensor.transpose(tp[:, q * P : (q + 1) * P], words[:, (4 * j + q) * P : (4 * j + q + 1) * P], ident[:])
+            dst = grp[i][:].bitcast(F32)[:, j * 512 : (j + 1) * 512].rearrange("p (a r u) -> p a r u", a=2, u=2)
+            src = tp[:].rearrange("p (a u r) -> p a r u", a=2, u=2)
+            if engine == "scalar":
+                nc.scalar.copy(out=dst, in_=src)
+            else:
+                nc.vector.tensor_copy(out=dst, in_=src)
+
+        def quantise(i):
+            kind, idx = blocks[i]
+            g = grp[i]
+            if kind == "x":
+                for w in range(W):
+                    cols = slice(w * N + idx * P, w * N + (idx + 1) * P)
+                    nc.vector.quantize_mx(out=xq[:, cols].bitcast(FP8X4), scales=xs[:, cols], in_=g[:, w * 512 : (w + 1) * 512])
+            else:
+                q = tq_pool.tile([P, W * P], U32, name="tq", align_bytes=64)
+                s = tq_pool.tile([P, W * P], U8, name="ts", align_bytes=64)
+                nc.vector.quantize_mx(out=q[:].bitcast(FP8X4), scales=s[:], in_=g[:])
+                tq[idx] = q
+                ts[idx] = s
+
+        s_ps = {}
+        c0 = {}
+        tanh = {}
+        yv = {}
+        du = {}
+        mx = {}
+        mm = {}
+        za = {}
+
+        def fill(r, b):
+            hb, c = r // 2, r % 2
+            s = ps_s.tile([P, 512], F32, name="s")
+            for a in range(2):
+                w = 2 * b + a
+                nc.tensor.matmul_mx(
+                    out=s[:, a * NC : (a + 1) * NC],
+                    lhsT=tq[hb][:, w * P : (w + 1) * P].bitcast(FP8X4),
+                    lhsT_scale=ts[hb][:, w * P : (w + 1) * P],
+                    rhs=xq[:, w * N + c * NC : w * N + (c + 1) * NC].bitcast(FP8X4),
+                    rhs_scale=xs[:, w * N + c * NC : w * N + (c + 1) * NC],
+                    start=True,
+                    stop=True,
+                )
+            s_ps[(r, b)] = s
+            if b == 0:
+                cp = m_pool.tile([P, 512], F32, name="c0")
+                nc.scalar.copy(out=cp[:], in_=s[:])
+                c0[r] = cp
+            t = t_pool.tile([P, 512], F32, name="tanh")
+            nc.scalar.activation(out=t[:], in_=s[:], func=ACT.Tanh, scale=0.5)
+            tanh[(r, b)] = t
+
+        def gate_and_max(r, b):
+            s = s_ps[(r, b)]
+            y = y_pool.tile([P, 512], F32, name="y")
+            nc.vector.scalar_tensor_tensor(out=y[:], in0=tanh[(r, b)][:], scalar=1.0, in1=s[:], op0=ALU.add, op1=ALU.mult)
+            yv[(r, b)] = y
+            if b == 1:
+                mx[r] = m_pool.tile([P, 512], F32, name="mx")
+                nc.vector.tensor_tensor(out=mx[r][:], in0=s[:], in1=c0[r][:], op=ALU.max)
+            elif b > 1:
+                nc.vector.tensor_tensor(out=mx[r][:], in0=s[:], in1=mx[r][:], op=ALU.max)
+            if b == BANKS - 1:
+                mm[r] = m_pool.tile([P, NC], F32, name="mm")
+                nc.vector.tensor_tensor(out=mm[r][:], in0=mx[r][:, 0:NC], in1=mx[r][:, NC : 2 * NC], op=ALU.max)
+
+        def weights(r, b):
+            s = s_ps[(r, b)]
+            d = u_pool.tile([P, 512], F32, name="u")
+            nc.vector.tensor_tensor(
+                out=d[:].rearrange("p (a n) -> p a n", a=2),
+                in0=s[:].rearrange("p (a n) -> p a n", a=2),
+                in1=mm[r][:].unsqueeze(1).to_broadcast([P, 2, NC]),
+                op=ALU.subtract,
+            )
+            nc.scalar.activation(out=d[:], in_=d[:], func=ACT.Exp)
+            du[(r, b)] = d
+            y = yv[(r, b)]
+            nc.gpsimd.tensor_tensor(out=y[:], in0=y[:], in1=d[:], op=ALU.mult)
+
+        def sums(r):
+            z = ps_za.tile([P, 512], F32, name="za")
+            for slot in range(4):
+                src = du if slot < 2 else yv
+                nb = slot % 2
+                for w in range(W):
+                    nc.tensor.matmul(
+                        out=z[:, slot * P : (slot + 1) * P],
+                        lhsT=src[(r, w // 2)][:, (w % 2) * NC + nb * P : (w % 2) * NC + (nb + 1) * P],
+                        rhs=ident[:],
+                        is_transpose=True,
+                        start=(w == 0),
+                        stop=(w == W - 1),
+                    )
+            za[r] = z
+
+        def finish(r):
+            hb, c = r // 2, r % 2
+            z = za[r]
+            rz = m_pool.tile([P, NC], F32, name="rz")
+            nc.vector.reciprocal(out=rz[:], in_=z[:, 0:NC])
+            nc.vector.scalar_tensor_tensor(
+                out=out_sb[:, 2 * c : 2 * c + 2, hb * P : (hb + 1) * P],
+                in0=z[:, NC : 2 * NC].rearrange("p (a h) -> p a h", a=2),
+                scalar=0.5,
+                in1=rz[:].rearrange("p (a h) -> p a h", a=2),
+                op0=ALU.mult,
+                op1=ALU.mult,
+            )
+            if hb % 4 == 3 and c == 1:
+                cols = slice((hb - 3) * P, (hb + 1) * P)
+                for nb in range(N // P):
+                    nc.sync.dma_start(out=out[nb * P : (nb + 1) * P, cols], in_=out_sb[:, nb, cols])
+
+        HEAD = 6
+        for i in range(HEAD):
+            load(i)
+        for i in range(HEAD):
+            for j in range(4):
+                transposes(i, j, "scalar" if j % 2 == 0 else "vector")
+            load(i + HEAD)
+            if i > 0:
+                quantise(i - 1)
+        quantise(HEAD - 1)
+
+        for r in range(-1, ROUNDS + 1):
+            nxt = r + 1 < ROUNDS
+            if nxt:
+                fill(r + 1, 0)
+            hb_t = (r + 4) // 2
+            i_t = hb_t + 4
+            if r >= 0 and hb_t < H // P:
+                for j in range(2):
+                    transposes(i_t, 2 * (r % 2) + j, "scalar")
+                if r % 2 == 1 and i_t + HEAD < len(blocks):
+                    load(i_t + HEAD)
+            if 0 <= r < ROUNDS:
+                for b in range(BANKS):
+                    gate_and_max(r, b)
+            if r >= 1:
+                sums(r - 1)
+            for b in range(BANKS):
+                if 0 <= r < ROUNDS:
+                    weights(r, b)
+                if nxt and b < BANKS - 1:
+                    fill(r + 1, b + 1)
+            if r >= 1:
+                finish(r - 1)
+            hb_q = (r + 2) // 2
+            if r >= 2 and r % 2 == 0 and hb_q < H // P:
+                quantise(hb_q + 4)

@@ -16,9 +16,12 @@ N, H, W, K = 512, 2048, 8, 512
 FLOPS = 2 * N * H * W * K
 
 NC = 256
-ROUNDS = (H // P) * (N // NC)
+HB = H // P
+NB = N // P
 BANKS = 4
-PINNED = False
+GROUP = 4
+GW = GROUP * P
+PINNED = True
 
 
 def tile_dendriticlayersilu_ffn_kernel(tc, x, template_flat, out):
@@ -28,12 +31,14 @@ def tile_dendriticlayersilu_ffn_kernel(tc, x, template_flat, out):
             ctx.enter_context(tc.manual_schedule())
         const = ctx.enter_context(tc.tile_pool(name="const", bufs=1))
         raw_pool = ctx.enter_context(tc.tile_pool(name="raw", bufs=6))
-        grp_pool = ctx.enter_context(tc.tile_pool(name="grp", bufs=2))
-        tq_pool = ctx.enter_context(tc.tile_pool(name="tq", bufs=3))
+        grp_pool = ctx.enter_context(tc.tile_pool(name="grp", bufs=3))
+        tq_pool = ctx.enter_context(tc.tile_pool(name="tq", bufs=6))
         t_pool = ctx.enter_context(tc.tile_pool(name="tanh", bufs=6))
         u_pool = ctx.enter_context(tc.tile_pool(name="u", bufs=12))
         y_pool = ctx.enter_context(tc.tile_pool(name="y", bufs=12))
+        c_pool = ctx.enter_context(tc.tile_pool(name="c", bufs=3))
         m_pool = ctx.enter_context(tc.tile_pool(name="m", bufs=2))
+        za_pool = ctx.enter_context(tc.tile_pool(name="za_sb", bufs=2))
         ps_s = ctx.enter_context(tc.psum_pool(name="ps_s", bufs=5))
         ps_za = ctx.enter_context(tc.psum_pool(name="ps_za", bufs=1))
         ps_tp = ctx.enter_context(tc.psum_pool(name="ps_tp", bufs=2))
@@ -42,20 +47,29 @@ def tile_dendriticlayersilu_ffn_kernel(tc, x, template_flat, out):
         make_identity(nc, ident[:])
         xq = const.tile([P, W * N], U32, name="xq", align_bytes=64)
         xs = const.tile([P, W * N], U8, name="xs", align_bytes=64)
-        out_sb = const.tile([P, N // P, H], F32, name="out_sb")
 
-        blocks = [("x", 0), ("x", 1), ("t", 0), ("x", 2), ("x", 3)] + [("t", i) for i in range(1, H // P)]
+        rounds = [(hb, c) for c in range(2) for hb in range(GROUP)] + [(hb, c) for hb in range(GROUP, HB) for c in range(2)]
+        n_rounds = len(rounds)
+
+        def live(r):
+            return 0 <= r < n_rounds
+
+        blocks = [("x", 0), ("x", 1), ("t", 0), ("t", 1), ("t", 2), ("t", 3), ("x", 2), ("x", 3)] + [("t", i) for i in range(GROUP, HB)]
+        depth = 6
         raw = {}
         grp = {}
         tq = {}
         ts = {}
 
-        def load(i):
+        def source(i):
             kind, idx = blocks[i]
             src = x if kind == "x" else template_flat
-            r = raw_pool.tile([P, W * K], BF16, name="raw")
-            nc.sync.dma_start(out=r[:], in_=src[idx * P : (idx + 1) * P, :])
-            raw[i] = r
+            return src[idx * P : (idx + 1) * P, :]
+
+        def load(i):
+            if i < len(blocks):
+                raw[i] = raw_pool.tile([P, W * K], BF16, name="raw")
+                nc.sync.dma_start(out=raw[i][:], in_=source(i))
 
         def transposes(i, j, engine):
             if j == 0:
@@ -70,20 +84,26 @@ def tile_dendriticlayersilu_ffn_kernel(tc, x, template_flat, out):
                 nc.scalar.copy(out=dst, in_=src)
             else:
                 nc.vector.tensor_copy(out=dst, in_=src)
+            if j == 3:
+                load(i + depth)
 
-        def quantise(i):
+        def quantise(i, j0, j1):
             kind, idx = blocks[i]
             g = grp[i]
             if kind == "x":
-                for w in range(W):
+                for w in range(2 * j0, 2 * j1):
                     cols = slice(w * N + idx * P, w * N + (idx + 1) * P)
                     nc.vector.quantize_mx(out=xq[:, cols].bitcast(FP8X4), scales=xs[:, cols], in_=g[:, w * 512 : (w + 1) * 512])
             else:
-                q = tq_pool.tile([P, W * P], U32, name="tq", align_bytes=64)
-                s = tq_pool.tile([P, W * P], U8, name="ts", align_bytes=64)
-                nc.vector.quantize_mx(out=q[:].bitcast(FP8X4), scales=s[:], in_=g[:])
-                tq[idx] = q
-                ts[idx] = s
+                if j0 == 0:
+                    tq[idx] = tq_pool.tile([P, W * P], U32, name="tq", align_bytes=64)
+                    ts[idx] = tq_pool.tile([P, W * P], U8, name="ts", align_bytes=64)
+                cols = slice(j0 * 2 * P, j1 * 2 * P)
+                nc.vector.quantize_mx(out=tq[idx][:, cols].bitcast(FP8X4), scales=ts[idx][:, cols], in_=g[:, j0 * 1024 : j1 * 1024])
+
+        def prepare(i):
+            for j in range(4):
+                transposes(i, j, "scalar" if j % 2 == 0 else "vector")
 
         s_ps = {}
         c0 = {}
@@ -93,9 +113,12 @@ def tile_dendriticlayersilu_ffn_kernel(tc, x, template_flat, out):
         mx = {}
         mm = {}
         za = {}
+        za_sb = {}
 
         def fill(r, b):
-            hb, c = r // 2, r % 2
+            if not live(r):
+                return
+            hb, c = rounds[r]
             s = ps_s.tile([P, 512], F32, name="s")
             for a in range(2):
                 w = 2 * b + a
@@ -109,15 +132,20 @@ def tile_dendriticlayersilu_ffn_kernel(tc, x, template_flat, out):
                     stop=True,
                 )
             s_ps[(r, b)] = s
+
+        def squash(r, b):
+            if not live(r):
+                return
+            s = s_ps[(r, b)]
             if b == 0:
-                cp = m_pool.tile([P, 512], F32, name="c0")
-                nc.scalar.copy(out=cp[:], in_=s[:])
-                c0[r] = cp
-            t = t_pool.tile([P, 512], F32, name="tanh")
-            nc.scalar.activation(out=t[:], in_=s[:], func=ACT.Tanh, scale=0.5)
-            tanh[(r, b)] = t
+                c0[r] = c_pool.tile([P, 512], F32, name="c0")
+                nc.scalar.copy(out=c0[r][:], in_=s[:])
+            tanh[(r, b)] = t_pool.tile([P, 512], F32, name="tanh")
+            nc.scalar.activation(out=tanh[(r, b)][:], in_=s[:], func=ACT.Tanh, scale=0.5)
 
         def gate_and_max(r, b):
+            if not live(r):
+                return
             s = s_ps[(r, b)]
             y = y_pool.tile([P, 512], F32, name="y")
             nc.vector.scalar_tensor_tensor(out=y[:], in0=tanh[(r, b)][:], scalar=1.0, in1=s[:], op0=ALU.add, op1=ALU.mult)
@@ -128,91 +156,160 @@ def tile_dendriticlayersilu_ffn_kernel(tc, x, template_flat, out):
             elif b > 1:
                 nc.vector.tensor_tensor(out=mx[r][:], in0=s[:], in1=mx[r][:], op=ALU.max)
             if b == BANKS - 1:
-                mm[r] = m_pool.tile([P, NC], F32, name="mm")
+                mm[r] = c_pool.tile([P, NC], F32, name="mm")
                 nc.vector.tensor_tensor(out=mm[r][:], in0=mx[r][:, 0:NC], in1=mx[r][:, NC : 2 * NC], op=ALU.max)
 
-        def weights(r, b):
-            s = s_ps[(r, b)]
+        def shift(r, b):
+            if not live(r):
+                return
             d = u_pool.tile([P, 512], F32, name="u")
-            nc.vector.tensor_tensor(
+            engine = nc.gpsimd if b == 0 else nc.vector
+            s = c0[r] if b == 0 else s_ps[(r, b)]
+            engine.tensor_tensor(
                 out=d[:].rearrange("p (a n) -> p a n", a=2),
                 in0=s[:].rearrange("p (a n) -> p a n", a=2),
                 in1=mm[r][:].unsqueeze(1).to_broadcast([P, 2, NC]),
                 op=ALU.subtract,
             )
-            nc.scalar.activation(out=d[:], in_=d[:], func=ACT.Exp)
             du[(r, b)] = d
-            y = yv[(r, b)]
-            nc.gpsimd.tensor_tensor(out=y[:], in0=y[:], in1=d[:], op=ALU.mult)
 
-        def sums(r):
-            z = ps_za.tile([P, 512], F32, name="za")
-            for slot in range(4):
-                src = du if slot < 2 else yv
-                nb = slot % 2
+        def exponent(r, b):
+            if live(r):
+                nc.scalar.activation(out=du[(r, b)][:], in_=du[(r, b)][:], func=ACT.Exp)
+
+        def product(r, b):
+            if live(r):
+                engine = nc.vector if (r == n_rounds - 1 and b % 2 == 1) else nc.gpsimd
+                engine.tensor_tensor(out=yv[(r, b)][:], in0=yv[(r, b)][:], in1=du[(r, b)][:], op=ALU.mult)
+
+        def sums(r, half):
+            if not live(r):
+                return
+            if half == 0:
+                za[r] = ps_za.tile([P, 512], F32, name="za")
+            src = yv if half else du
+            for nb in range(2):
+                slot = 2 * half + nb
                 for w in range(W):
                     nc.tensor.matmul(
-                        out=z[:, slot * P : (slot + 1) * P],
+                        out=za[r][:, slot * P : (slot + 1) * P],
                         lhsT=src[(r, w // 2)][:, (w % 2) * NC + nb * P : (w % 2) * NC + (nb + 1) * P],
                         rhs=ident[:],
                         is_transpose=True,
                         start=(w == 0),
                         stop=(w == W - 1),
                     )
-            za[r] = z
 
-        def finish(r):
-            hb, c = r // 2, r % 2
+        def store(g, nb, lo, hi):
+            nc.sync.dma_start(out=out[nb * P : (nb + 1) * P, g * GW + lo : g * GW + hi], in_=za_sb[g][:, 1, nb, lo:hi])
+
+        def width(g):
+            return GW if g < HB // GROUP - 1 else GW - P
+
+        def collect(r):
+            if not live(r):
+                return
+            hb, c = rounds[r]
+            g, hl = hb // GROUP, hb % GROUP
+            if g not in za_sb:
+                za_sb[g] = za_pool.tile([P, 2, NB, GW], F32, name="za_sb")
             z = za[r]
-            rz = m_pool.tile([P, NC], F32, name="rz")
-            nc.vector.reciprocal(out=rz[:], in_=z[:, 0:NC])
-            nc.vector.scalar_tensor_tensor(
-                out=out_sb[:, 2 * c : 2 * c + 2, hb * P : (hb + 1) * P],
-                in0=z[:, NC : 2 * NC].rearrange("p (a h) -> p a h", a=2),
-                scalar=0.5,
-                in1=rz[:].rearrange("p (a h) -> p a h", a=2),
-                op0=ALU.mult,
-                op1=ALU.mult,
-            )
-            if hb % 4 == 3 and c == 1:
-                cols = slice((hb - 3) * P, (hb + 1) * P)
-                for nb in range(N // P):
-                    nc.sync.dma_start(out=out[nb * P : (nb + 1) * P, cols], in_=out_sb[:, nb, cols])
+            cols = slice(hl * P, (hl + 1) * P)
+            if hb < HB - 1:
+                nc.scalar.copy(out=za_sb[g][:, :, 2 * c : 2 * c + 2, cols], in_=z[:].rearrange("p (z a h) -> p z a h", z=2, a=2))
+            else:
+                rz = m_pool.tile([P, NC], F32, name="rz")
+                nc.vector.reciprocal(out=rz[:], in_=z[:, 0:NC])
+                nc.vector.scalar_tensor_tensor(
+                    out=za_sb[g][:, 1, 2 * c : 2 * c + 2, cols],
+                    in0=z[:, NC : 2 * NC].rearrange("p (a h) -> p a h", a=2),
+                    scalar=0.5,
+                    in1=rz[:].rearrange("p (a h) -> p a h", a=2),
+                    op0=ALU.mult,
+                    op1=ALU.mult,
+                )
+                store(g, 2 * c, hl * P, (hl + 1) * P)
+                store(g, 2 * c + 1, hl * P, (hl + 1) * P)
 
-        HEAD = 6
-        for i in range(HEAD):
+        def logarithm(g):
+            zs = za_sb[g][:, 0, :, 0 : width(g)]
+            nc.scalar.activation(out=zs, in_=zs, func=ACT.Ln, scale=2.0)
+
+        def inverse(g, nb):
+            zs = za_sb[g][:, 0, nb, 0 : width(g)]
+            nc.scalar.activation(out=zs, in_=zs, func=ACT.Exp, scale=-1.0)
+
+        def scale(g, nb, engine):
+            a = za_sb[g][:, 1, nb, 0 : width(g)]
+            engine.tensor_tensor(out=a, in0=a, in1=za_sb[g][:, 0, nb, 0 : width(g)], op=ALU.mult)
+            store(g, nb, 0, width(g))
+
+        first = [0, 1, 2]
+        for i in first:
+            raw[i] = raw_pool.tile([P, W * K], BF16, name="raw")
+        for j in range(4):
+            for i in first:
+                nc.sync.dma_start(out=raw[i][:, j * 1024 : (j + 1) * 1024], in_=source(i)[:, j * 1024 : (j + 1) * 1024])
+        for i in range(len(first), depth):
             load(i)
-        for i in range(HEAD):
-            for j in range(4):
-                transposes(i, j, "scalar" if j % 2 == 0 else "vector")
-            load(i + HEAD)
-            if i > 0:
-                quantise(i - 1)
-        quantise(HEAD - 1)
+        for j in range(5):
+            if j < 4:
+                for n, i in enumerate(first):
+                    transposes(i, j, "scalar" if (3 * j + n) % 2 == 0 else "vector")
+            if j > 0:
+                for i in first:
+                    quantise(i, j - 1, j)
+                fill(0, j - 1)
+                squash(0, j - 1)
 
-        for r in range(-1, ROUNDS + 1):
-            nxt = r + 1 < ROUNDS
-            if nxt:
-                fill(r + 1, 0)
+        early = {-1: [3], 0: [4], 1: [5, 6], 2: [7]}
+        last_group = HB // GROUP - 1
+
+        for r in range(-1, n_rounds + 8):
+            if r >= 0:
+                squash(r + 1, 0)
+            gate_and_max(r, 0)
+            if r >= 0:
+                fill(r + 1, 1)
+                squash(r + 1, 1)
+            g, k = (r - 10) // 8, (r - 10) % 8
+            if 0 <= g < last_group and k == 0:
+                logarithm(g)
+            for b in range(1, BANKS):
+                gate_and_max(r, b)
+            sums(r - 2, 0)
+            for i in early.get(r, []):
+                prepare(i)
             hb_t = (r + 4) // 2
-            i_t = hb_t + 4
-            if r >= 0 and hb_t < H // P:
-                for j in range(2):
-                    transposes(i_t, 2 * (r % 2) + j, "scalar")
-                if r % 2 == 1 and i_t + HEAD < len(blocks):
-                    load(i_t + HEAD)
-            if 0 <= r < ROUNDS:
-                for b in range(BANKS):
-                    gate_and_max(r, b)
-            if r >= 1:
-                sums(r - 1)
+            if GROUP <= hb_t < HB:
+                transposes(hb_t + 4, 2 * (r % 2), "scalar")
+                transposes(hb_t + 4, 2 * (r % 2) + 1, "vector")
+            sums(r - 2, 1)
             for b in range(BANKS):
-                if 0 <= r < ROUNDS:
-                    weights(r, b)
-                if nxt and b < BANKS - 1:
-                    fill(r + 1, b + 1)
-            if r >= 1:
-                finish(r - 1)
-            hb_q = (r + 2) // 2
-            if r >= 2 and r % 2 == 0 and hb_q < H // P:
-                quantise(hb_q + 4)
+                exponent(r - 1, b)
+            collect(r - 2)
+            if r - 2 == n_rounds - 3:
+                logarithm(last_group)
+            if 0 <= g < last_group and 1 <= k <= NB:
+                inverse(g, k - 1)
+            if 0 <= g < last_group and 2 <= k <= NB + 1:
+                scale(g, k - 2, nc.gpsimd)
+            for b in range(BANKS):
+                product(r - 1, b)
+            if r == n_rounds:
+                for nb in range(NB):
+                    inverse(last_group, nb)
+                    scale(last_group, nb, nc.vector)
+            shift(r, 0)
+            for b in range(1, BANKS):
+                shift(r, b)
+                if b == BANKS - 1:
+                    for i in early.get(r, []):
+                        quantise(i, 0, 4)
+                    hb_q = (r + 2) // 2
+                    if r % 2 == 0 and GROUP <= hb_q < HB:
+                        quantise(hb_q + 4, 0, 4)
+                if r >= 0 or b == BANKS - 1:
+                    fill(r + 1 + b // (BANKS - 1), (b + 1) % BANKS)
+                if r >= 0 and b < BANKS - 1:
+                    squash(r + 1, b + 1)

@@ -22,6 +22,8 @@ BANKS = 4
 GROUP = 4
 GW = GROUP * P
 PINNED = True
+PIECES = 2
+WARM = [2, 4, 4]
 
 
 def tile_dendriticlayersilu_ffn_kernel(tc, x, template_flat, out):
@@ -34,8 +36,8 @@ def tile_dendriticlayersilu_ffn_kernel(tc, x, template_flat, out):
         grp_pool = ctx.enter_context(tc.tile_pool(name="grp", bufs=3))
         tq_pool = ctx.enter_context(tc.tile_pool(name="tq", bufs=6))
         t_pool = ctx.enter_context(tc.tile_pool(name="tanh", bufs=6))
-        u_pool = ctx.enter_context(tc.tile_pool(name="u", bufs=12))
-        y_pool = ctx.enter_context(tc.tile_pool(name="y", bufs=12))
+        u_pool = ctx.enter_context(tc.tile_pool(name="u", bufs=3))
+        y_pool = ctx.enter_context(tc.tile_pool(name="y", bufs=3))
         c_pool = ctx.enter_context(tc.tile_pool(name="c", bufs=3))
         m_pool = ctx.enter_context(tc.tile_pool(name="m", bufs=2))
         za_pool = ctx.enter_context(tc.tile_pool(name="za_sb", bufs=2))
@@ -115,12 +117,12 @@ def tile_dendriticlayersilu_ffn_kernel(tc, x, template_flat, out):
         za = {}
         za_sb = {}
 
-        def fill(r, b):
+        def fill(r, b, times=1):
             if not live(r):
                 return
             hb, c = rounds[r]
             s = ps_s.tile([P, 512], F32, name="s")
-            for a in range(2):
+            for a in [0, 1] * times:
                 w = 2 * b + a
                 nc.tensor.matmul_mx(
                     out=s[:, a * NC : (a + 1) * NC],
@@ -147,9 +149,11 @@ def tile_dendriticlayersilu_ffn_kernel(tc, x, template_flat, out):
             if not live(r):
                 return
             s = s_ps[(r, b)]
-            y = y_pool.tile([P, 512], F32, name="y")
-            nc.vector.scalar_tensor_tensor(out=y[:], in0=tanh[(r, b)][:], scalar=1.0, in1=s[:], op0=ALU.add, op1=ALU.mult)
-            yv[(r, b)] = y
+            if b == 0:
+                yv[r] = y_pool.tile([P, BANKS * 512], F32, name="y")
+            nc.vector.scalar_tensor_tensor(
+                out=yv[r][:, b * 512 : (b + 1) * 512], in0=tanh[(r, b)][:], scalar=1.0, in1=s[:], op0=ALU.add, op1=ALU.mult
+            )
             if b == 1:
                 mx[r] = m_pool.tile([P, 512], F32, name="mx")
                 nc.vector.tensor_tensor(out=mx[r][:], in0=s[:], in1=c0[r][:], op=ALU.max)
@@ -162,43 +166,60 @@ def tile_dendriticlayersilu_ffn_kernel(tc, x, template_flat, out):
         def shift(r, b):
             if not live(r):
                 return
-            d = u_pool.tile([P, 512], F32, name="u")
+            if b == 0:
+                du[r] = u_pool.tile([P, BANKS * 512], F32, name="u")
+            d = du[r][:, b * 512 : (b + 1) * 512]
             engine = nc.gpsimd if b == 0 else nc.vector
             s = c0[r] if b == 0 else s_ps[(r, b)]
             engine.tensor_tensor(
-                out=d[:].rearrange("p (a n) -> p a n", a=2),
+                out=d.rearrange("p (a n) -> p a n", a=2),
                 in0=s[:].rearrange("p (a n) -> p a n", a=2),
                 in1=mm[r][:].unsqueeze(1).to_broadcast([P, 2, NC]),
                 op=ALU.subtract,
             )
-            du[(r, b)] = d
 
-        def exponent(r, b):
+        def piece(i):
+            return slice(i * BANKS * 512 // PIECES, (i + 1) * BANKS * 512 // PIECES)
+
+        def exponent(r, i):
             if live(r):
-                nc.scalar.activation(out=du[(r, b)][:], in_=du[(r, b)][:], func=ACT.Exp)
+                nc.scalar.activation(out=du[r][:, piece(i)], in_=du[r][:, piece(i)], func=ACT.Exp)
 
-        def product(r, b):
+        def product(r, i):
             if live(r):
-                engine = nc.vector if (r == n_rounds - 1 and b % 2 == 1) else nc.gpsimd
-                engine.tensor_tensor(out=yv[(r, b)][:], in0=yv[(r, b)][:], in1=du[(r, b)][:], op=ALU.mult)
+                engine = nc.vector if (r == n_rounds - 1 and i % 2 == 1) else nc.gpsimd
+                engine.tensor_tensor(out=yv[r][:, piece(i)], in0=yv[r][:, piece(i)], in1=du[r][:, piece(i)], op=ALU.mult)
 
-        def sums(r, half):
+        def warm(r, n):
             if not live(r):
                 return
-            if half == 0:
+            for i in range(n):
+                nc.tensor.matmul_mx(
+                    out=za[r][:, NC : 2 * NC],
+                    lhsT=xq[:, 0:P].bitcast(FP8X4),
+                    lhsT_scale=xs[:, 0:P],
+                    rhs=xq[:, 0:NC].bitcast(FP8X4),
+                    rhs_scale=xs[:, 0:NC],
+                    start=True,
+                    stop=True,
+                )
+
+        def sums(r, half, nb):
+            if not live(r):
+                return
+            if half == 0 and nb == 0:
                 za[r] = ps_za.tile([P, 512], F32, name="za")
-            src = yv if half else du
-            for nb in range(2):
-                slot = 2 * half + nb
-                for w in range(W):
-                    nc.tensor.matmul(
-                        out=za[r][:, slot * P : (slot + 1) * P],
-                        lhsT=src[(r, w // 2)][:, (w % 2) * NC + nb * P : (w % 2) * NC + (nb + 1) * P],
-                        rhs=ident[:],
-                        is_transpose=True,
-                        start=(w == 0),
-                        stop=(w == W - 1),
-                    )
+            src = yv[r] if half else du[r]
+            slot = 2 * half + nb
+            for w in range(W):
+                nc.tensor.matmul(
+                    out=za[r][:, slot * P : (slot + 1) * P],
+                    lhsT=src[:, w * NC + nb * P : w * NC + (nb + 1) * P],
+                    rhs=ident[:],
+                    is_transpose=True,
+                    start=(w == 0),
+                    stop=(w == W - 1),
+                )
 
         def store(g, nb, lo, hi):
             nc.sync.dma_start(out=out[nb * P : (nb + 1) * P, g * GW + lo : g * GW + hi], in_=za_sb[g][:, 1, nb, lo:hi])
@@ -252,41 +273,50 @@ def tile_dendriticlayersilu_ffn_kernel(tc, x, template_flat, out):
                 nc.sync.dma_start(out=raw[i][:, j * 1024 : (j + 1) * 1024], in_=source(i)[:, j * 1024 : (j + 1) * 1024])
         for i in range(len(first), depth):
             load(i)
-        for j in range(5):
+        for j in range(6):
             if j < 4:
                 for n, i in enumerate(first):
                     transposes(i, j, "scalar" if (3 * j + n) % 2 == 0 else "vector")
-            if j > 0:
+            if 1 <= j <= 4:
                 for i in first:
                     quantise(i, j - 1, j)
                 fill(0, j - 1)
                 squash(0, j - 1)
+            if j >= 2:
+                gate_and_max(0, j - 2)
 
-        early = {-1: [3], 0: [4], 1: [5, 6], 2: [7]}
+        early = {0: [4], 1: [5, 6], 2: [7]}
         last_group = HB // GROUP - 1
 
-        for r in range(-1, n_rounds + 8):
-            if r >= 0:
-                squash(r + 1, 0)
-            gate_and_max(r, 0)
-            if r >= 0:
-                fill(r + 1, 1)
-                squash(r + 1, 1)
+        for r in range(n_rounds + 8):
+            if r == 0:
+                prepare(3)
+                quantise(3, 0, 4)
+                fill(1, 0)
+            squash(r + 1, 0)
+            if r > 0:
+                gate_and_max(r, 0)
+            fill(r + 1, 1, WARM[0])
+            squash(r + 1, 1)
             g, k = (r - 10) // 8, (r - 10) % 8
             if 0 <= g < last_group and k == 0:
                 logarithm(g)
-            for b in range(1, BANKS):
-                gate_and_max(r, b)
-            sums(r - 2, 0)
-            for i in early.get(r, []):
-                prepare(i)
+            if r > 0:
+                for b in range(1, BANKS):
+                    gate_and_max(r, b)
             hb_t = (r + 4) // 2
+            sums(r - 2, 0, 0)
             if GROUP <= hb_t < HB:
                 transposes(hb_t + 4, 2 * (r % 2), "scalar")
+            warm(r - 2, WARM[1])
+            sums(r - 2, 0, 1)
+            if GROUP <= hb_t < HB:
                 transposes(hb_t + 4, 2 * (r % 2) + 1, "vector")
-            sums(r - 2, 1)
-            for b in range(BANKS):
-                exponent(r - 1, b)
+            warm(r - 2, WARM[2])
+            sums(r - 2, 1, 0)
+            sums(r - 2, 1, 1)
+            for i in range(PIECES):
+                exponent(r - 1, i)
             collect(r - 2)
             if r - 2 == n_rounds - 3:
                 logarithm(last_group)
@@ -294,8 +324,8 @@ def tile_dendriticlayersilu_ffn_kernel(tc, x, template_flat, out):
                 inverse(g, k - 1)
             if 0 <= g < last_group and 2 <= k <= NB + 1:
                 scale(g, k - 2, nc.gpsimd)
-            for b in range(BANKS):
-                product(r - 1, b)
+            for i in range(PIECES):
+                product(r - 1, i)
             if r == n_rounds:
                 for nb in range(NB):
                     inverse(last_group, nb)
@@ -305,11 +335,12 @@ def tile_dendriticlayersilu_ffn_kernel(tc, x, template_flat, out):
                 shift(r, b)
                 if b == BANKS - 1:
                     for i in early.get(r, []):
+                        prepare(i)
+                    for i in early.get(r, []):
                         quantise(i, 0, 4)
                     hb_q = (r + 2) // 2
                     if r % 2 == 0 and GROUP <= hb_q < HB:
                         quantise(hb_q + 4, 0, 4)
-                if r >= 0 or b == BANKS - 1:
-                    fill(r + 1 + b // (BANKS - 1), (b + 1) % BANKS)
-                if r >= 0 and b < BANKS - 1:
+                fill(r + 1 + b // (BANKS - 1), (b + 1) % BANKS)
+                if b < BANKS - 1:
                     squash(r + 1, b + 1)

@@ -22,6 +22,9 @@ BANKS = 4
 GROUP = 4
 GW = GROUP * P
 PINNED = True
+SUB0 = "gpsimd"
+SCALE = "gpsimd"
+TPC = ["vector", "vector"]
 PIECES = 2
 WARM = [2, 4, 4]
 
@@ -169,7 +172,7 @@ def tile_dendriticlayersilu_ffn_kernel(tc, x, template_flat, out):
             if b == 0:
                 du[r] = u_pool.tile([P, BANKS * 512], F32, name="u")
             d = du[r][:, b * 512 : (b + 1) * 512]
-            engine = nc.gpsimd if b == 0 else nc.vector
+            engine = nc.gpsimd if (b == 0 and SUB0 == "gpsimd") else nc.vector
             s = c0[r] if b == 0 else s_ps[(r, b)]
             engine.tensor_tensor(
                 out=d.rearrange("p (a n) -> p a n", a=2),
@@ -307,11 +310,11 @@ def tile_dendriticlayersilu_ffn_kernel(tc, x, template_flat, out):
             hb_t = (r + 4) // 2
             sums(r - 2, 0, 0)
             if GROUP <= hb_t < HB:
-                transposes(hb_t + 4, 2 * (r % 2), "scalar")
+                transposes(hb_t + 4, 2 * (r % 2), TPC[0])
             warm(r - 2, WARM[1])
             sums(r - 2, 0, 1)
             if GROUP <= hb_t < HB:
-                transposes(hb_t + 4, 2 * (r % 2) + 1, "vector")
+                transposes(hb_t + 4, 2 * (r % 2) + 1, TPC[1])
             warm(r - 2, WARM[2])
             sums(r - 2, 1, 0)
             sums(r - 2, 1, 1)
@@ -323,7 +326,7 @@ def tile_dendriticlayersilu_ffn_kernel(tc, x, template_flat, out):
             if 0 <= g < last_group and 1 <= k <= NB:
                 inverse(g, k - 1)
             if 0 <= g < last_group and 2 <= k <= NB + 1:
-                scale(g, k - 2, nc.gpsimd)
+                scale(g, k - 2, nc.gpsimd if SCALE == "gpsimd" else nc.vector)
             for i in range(PIECES):
                 product(r - 1, i)
             if r == n_rounds:

from contextlib import ExitStack

import concourse.mybir as mybir
from concourse.masks import make_identity

FP8X4 = mybir.dt.float8_e4m3fn_x4
BF16 = mybir.dt.bfloat16
F32 = mybir.dt.float32
U32 = mybir.dt.uint32
U8 = mybir.dt.uint8
ACT = mybir.ActivationFunctionType
ALU = mybir.AluOpType

P = 128
N, H, W, K = 512, 2048, 8, 512
FLOPS = 2 * N * H * W * K

NC = 256
HB = H // P
NB = N // P
BANKS = 4
GROUP = 4
GW = GROUP * P
PINNED = True
SUB0 = "gpsimd"
SCALE = "gpsimd"
TPC = ["vector", "vector"]
PIECES = 2
WARM = [2, 4, 4]


def tile_dendriticlayersilu_ffn_kernel(tc, x, template_flat, out):
    nc = tc.nc
    with ExitStack() as ctx:
        if PINNED:
            ctx.enter_context(tc.manual_schedule())
        const = ctx.enter_context(tc.tile_pool(name="const", bufs=1))
        raw_pool = ctx.enter_context(tc.tile_pool(name="raw", bufs=6))
        grp_pool = ctx.enter_context(tc.tile_pool(name="grp", bufs=3))
        tq_pool = ctx.enter_context(tc.tile_pool(name="tq", bufs=6))
        t_pool = ctx.enter_context(tc.tile_pool(name="tanh", bufs=6))
        u_pool = ctx.enter_context(tc.tile_pool(name="u", bufs=3))
        y_pool = ctx.enter_context(tc.tile_pool(name="y", bufs=3))
        c_pool = ctx.enter_context(tc.tile_pool(name="c", bufs=3))
        m_pool = ctx.enter_context(tc.tile_pool(name="m", bufs=2))
        za_pool = ctx.enter_context(tc.tile_pool(name="za_sb", bufs=2))
        ps_s = ctx.enter_context(tc.psum_pool(name="ps_s", bufs=5))
        ps_za = ctx.enter_context(tc.psum_pool(name="ps_za", bufs=1))
        ps_tp = ctx.enter_context(tc.psum_pool(name="ps_tp", bufs=2))

        ident = const.tile([P, P], F32, name="ident")
        make_identity(nc, ident[:])
        xq = const.tile([P, W * N], U32, name="xq", align_bytes=64)
        xs = const.tile([P, W * N], U8, name="xs", align_bytes=64)

        rounds = [(hb, c) for c in range(2) for hb in range(GROUP)] + [(hb, c) for hb in range(GROUP, HB) for c in range(2)]
        n_rounds = len(rounds)

        def live(r):
            return 0 <= r < n_rounds

        blocks = [("x", 0), ("x", 1), ("t", 0), ("t", 1), ("t", 2), ("t", 3), ("x", 2), ("x", 3)] + [("t", i) for i in range(GROUP, HB)]
        depth = 6
        raw = {}
        grp = {}
        tq = {}
        ts = {}

        def source(i):
            kind, idx = blocks[i]
            src = x if kind == "x" else template_flat
            return src[idx * P : (idx + 1) * P, :]

        def load(i):
            if i < len(blocks):
                raw[i] = raw_pool.tile([P, W * K], BF16, name="raw")
                nc.sync.dma_start(out=raw[i][:], in_=source(i))

        def transposes(i, j, engine):
            if j == 0:
                grp[i] = grp_pool.tile([P, W * K], BF16, name="grp", align_bytes=64)
            words = raw[i][:].bitcast(F32)
            tp = ps_tp.tile([P, 512], F32, name="tp")
            for q in range(4):
                nc.tensor.transpose(tp[:, q * P : (q + 1) * P], words[:, (4 * j + q) * P : (4 * j + q + 1) * P], ident[:])
            dst = grp[i][:].bitcast(F32)[:, j * 512 : (j + 1) * 512].rearrange("p (a r u) -> p a r u", a=2, u=2)
            src = tp[:].rearrange("p (a u r) -> p a r u", a=2, u=2)
            if engine == "scalar":
                nc.scalar.copy(out=dst, in_=src)
            else:
                nc.vector.tensor_copy(out=dst, in_=src)
            if j == 3:
                load(i + depth)

        def quantise(i, j0, j1):
            kind, idx = blocks[i]
            g = grp[i]
            if kind == "x":
                for w in range(2 * j0, 2 * j1):
                    cols = slice(w * N + idx * P, w * N + (idx + 1) * P)
                    nc.vector.quantize_mx(out=xq[:, cols].bitcast(FP8X4), scales=xs[:, cols], in_=g[:, w * 512 : (w + 1) * 512])
            else:
                if j0 == 0:
                    tq[idx] = tq_pool.tile([P, W * P], U32, name="tq", align_bytes=64)
                    ts[idx] = tq_pool.tile([P, W * P], U8, name="ts", align_bytes=64)
                cols = slice(j0 * 2 * P, j1 * 2 * P)
                nc.vector.quantize_mx(out=tq[idx][:, cols].bitcast(FP8X4), scales=ts[idx][:, cols], in_=g[:, j0 * 1024 : j1 * 1024])

        def prepare(i):
            for j in range(4):
                transposes(i, j, "scalar" if j % 2 == 0 else "vector")

        s_ps = {}
        c0 = {}
        tanh = {}
        yv = {}
        du = {}
        mx = {}
        mm = {}
        za = {}
        za_sb = {}

        def fill(r, b, times=1):
            if not live(r):
                return
            hb, c = rounds[r]
            s = ps_s.tile([P, 512], F32, name="s")
            for a in [0, 1] * times:
                w = 2 * b + a
                nc.tensor.matmul_mx(
                    out=s[:, a * NC : (a + 1) * NC],
                    lhsT=tq[hb][:, w * P : (w + 1) * P].bitcast(FP8X4),
                    lhsT_scale=ts[hb][:, w * P : (w + 1) * P],
                    rhs=xq[:, w * N + c * NC : w * N + (c + 1) * NC].bitcast(FP8X4),
                    rhs_scale=xs[:, w * N + c * NC : w * N + (c + 1) * NC],
                    start=True,
                    stop=True,
                )
            s_ps[(r, b)] = s

        def squash(r, b):
            if not live(r):
                return
            s = s_ps[(r, b)]
            if b == 0:
                c0[r] = c_pool.tile([P, 512], F32, name="c0")
                nc.scalar.copy(out=c0[r][:], in_=s[:])
            tanh[(r, b)] = t_pool.tile([P, 512], F32, name="tanh")
            nc.scalar.activation(out=tanh[(r, b)][:], in_=s[:], func=ACT.Tanh, scale=0.5)

        def gate_and_max(r, b):
            if not live(r):
                return
            s = s_ps[(r, b)]
            if b == 0:
                yv[r] = y_pool.tile([P, BANKS * 512], F32, name="y")
            nc.vector.scalar_tensor_tensor(
                out=yv[r][:, b * 512 : (b + 1) * 512], in0=tanh[(r, b)][:], scalar=1.0, in1=s[:], op0=ALU.add, op1=ALU.mult
            )
            if b == 1:
                mx[r] = m_pool.tile([P, 512], F32, name="mx")
                nc.vector.tensor_tensor(out=mx[r][:], in0=s[:], in1=c0[r][:], op=ALU.max)
            elif b > 1:
                nc.vector.tensor_tensor(out=mx[r][:], in0=s[:], in1=mx[r][:], op=ALU.max)
            if b == BANKS - 1:
                mm[r] = c_pool.tile([P, NC], F32, name="mm")
                nc.vector.tensor_tensor(out=mm[r][:], in0=mx[r][:, 0:NC], in1=mx[r][:, NC : 2 * NC], op=ALU.max)

        def shift(r, b):
            if not live(r):
                return
            if b == 0:
                du[r] = u_pool.tile([P, BANKS * 512], F32, name="u")
            d = du[r][:, b * 512 : (b + 1) * 512]
            engine = nc.gpsimd if (b == 0 and SUB0 == "gpsimd") else nc.vector
            s = c0[r] if b == 0 else s_ps[(r, b)]
            engine.tensor_tensor(
                out=d.rearrange("p (a n) -> p a n", a=2),
                in0=s[:].rearrange("p (a n) -> p a n", a=2),
                in1=mm[r][:].unsqueeze(1).to_broadcast([P, 2, NC]),
                op=ALU.subtract,
            )

        def piece(i):
            return slice(i * BANKS * 512 // PIECES, (i + 1) * BANKS * 512 // PIECES)

        def exponent(r, i):
            if live(r):
                nc.scalar.activation(out=du[r][:, piece(i)], in_=du[r][:, piece(i)], func=ACT.Exp)

        def product(r, i):
            if live(r):
                engine = nc.vector if (r == n_rounds - 1 and i % 2 == 1) else nc.gpsimd
                engine.tensor_tensor(out=yv[r][:, piece(i)], in0=yv[r][:, piece(i)], in1=du[r][:, piece(i)], op=ALU.mult)

        def warm(r, n):
            if not live(r):
                return
            for i in range(n):
                nc.tensor.matmul_mx(
                    out=za[r][:, NC : 2 * NC],
                    lhsT=xq[:, 0:P].bitcast(FP8X4),
                    lhsT_scale=xs[:, 0:P],
                    rhs=xq[:, 0:NC].bitcast(FP8X4),
                    rhs_scale=xs[:, 0:NC],
                    start=True,
                    stop=True,
                )

        def sums(r, half, nb):
            if not live(r):
                return
            if half == 0 and nb == 0:
                za[r] = ps_za.tile([P, 512], F32, name="za")
            src = yv[r] if half else du[r]
            slot = 2 * half + nb
            for w in range(W):
                nc.tensor.matmul(
                    out=za[r][:, slot * P : (slot + 1) * P],
                    lhsT=src[:, w * NC + nb * P : w * NC + (nb + 1) * P],
                    rhs=ident[:],
                    is_transpose=True,
                    start=(w == 0),
                    stop=(w == W - 1),
                )

        def store(g, nb, lo, hi):
            nc.sync.dma_start(out=out[nb * P : (nb + 1) * P, g * GW + lo : g * GW + hi], in_=za_sb[g][:, 1, nb, lo:hi])

        def width(g):
            return GW if g < HB // GROUP - 1 else GW - P

        def collect(r):
            if not live(r):
                return
            hb, c = rounds[r]
            g, hl = hb // GROUP, hb % GROUP
            if g not in za_sb:
                za_sb[g] = za_pool.tile([P, 2, NB, GW], F32, name="za_sb")
            z = za[r]
            cols = slice(hl * P, (hl + 1) * P)
            if hb < HB - 1:
                nc.scalar.copy(out=za_sb[g][:, :, 2 * c : 2 * c + 2, cols], in_=z[:].rearrange("p (z a h) -> p z a h", z=2, a=2))
            else:
                rz = m_pool.tile([P, NC], F32, name="rz")
                nc.vector.reciprocal(out=rz[:], in_=z[:, 0:NC])
                nc.vector.scalar_tensor_tensor(
                    out=za_sb[g][:, 1, 2 * c : 2 * c + 2, cols],
                    in0=z[:, NC : 2 * NC].rearrange("p (a h) -> p a h", a=2),
                    scalar=0.5,
                    in1=rz[:].rearrange("p (a h) -> p a h", a=2),
                    op0=ALU.mult,
                    op1=ALU.mult,
                )
                store(g, 2 * c, hl * P, (hl + 1) * P)
                store(g, 2 * c + 1, hl * P, (hl + 1) * P)

        def logarithm(g):
            zs = za_sb[g][:, 0, :, 0 : width(g)]
            nc.scalar.activation(out=zs, in_=zs, func=ACT.Ln, scale=2.0)

        def inverse(g, nb):
            zs = za_sb[g][:, 0, nb, 0 : width(g)]
            nc.scalar.activation(out=zs, in_=zs, func=ACT.Exp, scale=-1.0)

        def scale(g, nb, engine):
            a = za_sb[g][:, 1, nb, 0 : width(g)]
            engine.tensor_tensor(out=a, in0=a, in1=za_sb[g][:, 0, nb, 0 : width(g)], op=ALU.mult)
            store(g, nb, 0, width(g))

        first = [0, 1, 2]
        for i in first:
            raw[i] = raw_pool.tile([P, W * K], BF16, name="raw")
        for j in range(4):
            for i in first:
                nc.sync.dma_start(out=raw[i][:, j * 1024 : (j + 1) * 1024], in_=source(i)[:, j * 1024 : (j + 1) * 1024])
        for i in range(len(first), depth):
            load(i)
        for j in range(6):
            if j < 4:
                for n, i in enumerate(first):
                    transposes(i, j, "scalar" if (3 * j + n) % 2 == 0 else "vector")
            if 1 <= j <= 4:
                for i in first:
                    quantise(i, j - 1, j)
                fill(0, j - 1)
                squash(0, j - 1)
            if j >= 2:
                gate_and_max(0, j - 2)

        early = {0: [4], 1: [5, 6], 2: [7]}
        last_group = HB // GROUP - 1

        for r in range(n_rounds + 8):
            if r == 0:
                prepare(3)
                quantise(3, 0, 4)
                fill(1, 0)
            squash(r + 1, 0)
            if r > 0:
                gate_and_max(r, 0)
            fill(r + 1, 1, WARM[0])
            squash(r + 1, 1)
            g, k = (r - 10) // 8, (r - 10) % 8
            if 0 <= g < last_group and k == 0:
                logarithm(g)
            if r > 0:
                for b in range(1, BANKS):
                    gate_and_max(r, b)
            hb_t = (r + 4) // 2
            sums(r - 2, 0, 0)
            if GROUP <= hb_t < HB:
                transposes(hb_t + 4, 2 * (r % 2), TPC[0])
            warm(r - 2, WARM[1])
            sums(r - 2, 0, 1)
            if GROUP <= hb_t < HB:
                transposes(hb_t + 4, 2 * (r % 2) + 1, TPC[1])
            warm(r - 2, WARM[2])
            sums(r - 2, 1, 0)
            sums(r - 2, 1, 1)
            for i in range(PIECES):
                exponent(r - 1, i)
            collect(r - 2)
            if r - 2 == n_rounds - 3:
                logarithm(last_group)
            if 0 <= g < last_group and 1 <= k <= NB:
                inverse(g, k - 1)
            if 0 <= g < last_group and 2 <= k <= NB + 1:
                scale(g, k - 2, nc.gpsimd if SCALE == "gpsimd" else nc.vector)
            for i in range(PIECES):
                product(r - 1, i)
            if r == n_rounds:
                for nb in range(NB):
                    inverse(last_group, nb)
                    scale(last_group, nb, nc.vector)
            shift(r, 0)
            for b in range(1, BANKS):
                shift(r, b)
                if b == BANKS - 1:
                    for i in early.get(r, []):
                        prepare(i)
                    for i in early.get(r, []):
                        quantise(i, 0, 4)
                    hb_q = (r + 2) // 2
                    if r % 2 == 0 and GROUP <= hb_q < HB:
                        quantise(hb_q + 4, 0, 4)
                fill(r + 1 + b // (BANKS - 1), (b + 1) % BANKS)
                if b < BANKS - 1:
                    squash(r + 1, b + 1)
